import numpy as np
import ml_dtypes


def mxq(x, axis, fmt="e4m3"):
    dtype, down = {"e4m3": (ml_dtypes.float8_e4m3fn, 7), "e5m2": (ml_dtypes.float8_e5m2, 14)}[fmt]
    v = np.moveaxis(np.asarray(x, np.float32).astype(ml_dtypes.bfloat16).astype(np.float64), axis, -1)
    blocks = v.reshape(v.shape[:-1] + (-1, 32))
    amax = np.abs(blocks).max(-1, keepdims=True)
    byte = np.maximum(np.where(amax > 0, np.frexp(amax)[1] - 1 + 127, 0) - down, 1)
    scale = np.exp2(byte - 127.0)
    codes = (blocks / scale).astype(np.float32).astype(dtype).astype(np.float64)
    return np.moveaxis((codes * scale).reshape(v.shape), -1, axis)


WIDE = False


def mx_kscale(k):
    if not WIDE:
        return np.ones(k)
    levels = np.array([10, -10, 5, -5, 0])
    a = np.random.permutation(np.resize(levels, k // 512 * 4)).reshape(k // 512, 4)
    idx = np.arange(k)
    return np.exp2(a[idx // 512, idx % 128 // 32])


BF16 = ml_dtypes.bfloat16


def bf(x):
    return np.asarray(x, np.float32).astype(BF16)


def f64(x):
    return np.asarray(x).astype(np.float64)


N, M, E, F, Z = 16, 256, 1024, 512, 128


def embed(xq, w1q, b1, w2q, b2):
    h = np.maximum((xq @ w1q) + b1, 0.0)
    return np.maximum((mxq(h, 2, "e4m3") @ w2q) + b2, 0.0)


def setup_inputs():
    s, t = mx_kscale(E), mx_kscale(F)
    return {"xp1": bf(np.random.standard_normal((N, M, E)) * s),
            "xp2": bf(np.random.standard_normal((N, M, E)) * s),
            "W1": bf(np.random.standard_normal((E, F)) / np.sqrt(E) / s[:, None] * t),
            "b1": bf(np.random.standard_normal(F) * 0.3 * t),
            "W2": bf(np.random.standard_normal((F, Z)) * 2.0 / np.sqrt(F) / t[:, None]),
            "b2": bf(np.random.standard_normal(Z) * 0.3),
            "q_energy": bf(1.0 + 0.25 * np.random.standard_normal((N, M)))}


def reference(xp1, xp2, W1, b1, W2, b2, q_energy):
    w1q = mxq(f64(W1), 0, "e4m3")
    w2q = mxq(f64(W2), 0, "e4m3")
    z1 = embed(mxq(f64(xp1), 2, "e4m3"), w1q, f64(b1), w2q, f64(b2))
    z2 = embed(mxq(f64(xp2), 2, "e4m3"), w1q, f64(b1), w2q, f64(b2))
    d = z1 - z2
    return f64(q_energy) * np.mean(d * d, axis=2)

@@ -1,0 +1,259 @@
+from contextlib import ExitStack
+
+import concourse.mybir as mybir
+from concourse.masks import make_identity
+
+F32 = mybir.dt.float32
+BF16 = mybir.dt.bfloat16
+U32 = mybir.dt.uint32
+U8 = mybir.dt.uint8
+FP8X4 = mybir.dt.float8_e4m3fn_x4
+ACT = mybir.ActivationFunctionType
+ALU = mybir.AluOpType
+
+P = 128
+E = 1024
+F = 512
+Z = 128
+ROWS = 4096
+J = ROWS // P
+ROUNDS = 16
+
+FLOPS = 2 * 2 * ROWS * (E * F + F * Z)
+
+
+def tile_querysiamese_pa_t_kernel(tc, xp1, xp2, W1, b1, W2, b2, q_energy, out):
+    nc = tc.nc
+    with ExitStack() as ctx:
+        keep = ctx.enter_context(tc.tile_pool(name="keep", bufs=1))
+        work = ctx.enter_context(tc.tile_pool(name="work", bufs=2))
+        psx = ctx.enter_context(tc.psum_pool(name="psx", bufs=1))
+        psh = ctx.enter_context(tc.psum_pool(name="psh", bufs=3))
+        psz = ctx.enter_context(tc.psum_pool(name="psz", bufs=1))
+        ctx.enter_context(tc.manual_schedule())
+
+        xv = [
+            xp.rearrange("n m k -> (n m) k").rearrange("(p j) k -> p j k", j=J)
+            for xp in (xp1, xp2)
+        ]
+
+        b1r = keep.tile([P, 4], BF16, name="b1r")
+        nc.scalar.dma_start(out=b1r[:], in_=b1.rearrange("(p t) -> p t", t=4))
+        w2r = keep.tile([P, 4 * Z], BF16, name="w2r")
+        nc.scalar.dma_start(out=w2r[:], in_=W2.rearrange("(p t) z -> p (t z)", t=4))
+        b2r = keep.tile([P, Z], BF16, name="b2r")
+        nc.scalar.dma_start(out=b2r[:], in_=b2.partition_broadcast(P))
+        qr = keep.tile([P, J], BF16, name="qr")
+        nc.scalar.dma_start(
+            out=qr[:], in_=q_energy.rearrange("n m -> (n m)").rearrange("(p j) -> p j", j=J)
+        )
+
+        w1v = W1.rearrange("(c p e) f -> p c (e f)", c=4, p=P, e=2)
+        w1r = keep.tile([P, 8 * F], BF16, name="w1r")
+        for g in range(2):
+            nc.sync.dma_start(
+                out=w1r[:, g * 2048 : (g + 1) * 2048].rearrange("p (u x) -> p u x", u=2),
+                in_=w1v[:, 2 * g : 2 * g + 2, :],
+            )
+        xin = {}
+        for s in range(ROUNDS):
+            for a in range(2):
+                xt_in = keep.tile([P, 2 * E], BF16, name="x%d_%d" % (a, s))
+                nc.sync.dma_start(
+                    out=xt_in[:].rearrange("p (j k) -> p j k", j=2),
+                    in_=xv[a][:, 2 * s : 2 * s + 2, :],
+                )
+                xin[(a, s)] = xt_in
+
+        ident = keep.tile([P, P], F32, name="ident")
+        make_identity(nc, ident[:])
+
+        b1f = keep.tile([P, 4], F32, name="b1f")
+        nc.vector.tensor_copy(out=b1f[:], in_=b1r[:])
+        negb2 = keep.tile([P, Z], F32, name="negb2")
+        nc.vector.tensor_scalar(out=negb2[:], in0=b2r[:], scalar1=-1.0, scalar2=None, op0=ALU.mult)
+        qf = keep.tile([P, J], F32, name="qf")
+        nc.vector.tensor_copy(out=qf[:], in_=qr[:])
+        w2g = keep.tile([P, 4 * Z], BF16, name="w2g", align_bytes=64)
+        nc.vector.tensor_copy(
+            out=w2g[:].rearrange("p (z t) -> p z t", t=4),
+            in_=w2r[:].rearrange("p (t z) -> p z t", t=4),
+        )
+        w2c = keep.tile([P, Z], U32, name="w2c", align_bytes=64)
+        w2s = keep.tile([P, Z], U8, name="w2s", align_bytes=64)
+
+        w1g = keep.tile([P, 8 * F], BF16, name="w1g", align_bytes=64)
+        w1c = keep.tile([P, 2 * F], U32, name="w1c", align_bytes=64)
+        w1s = keep.tile([P, 2 * F], U8, name="w1s", align_bytes=64)
+
+        def w1_regroup(eng_copy, g, t0, t1):
+            dst = w1g[:, g * 2048 : (g + 1) * 2048].rearrange("p (t m j) -> p t m j", t=4, m=P, j=4)
+            src = w1r[:, g * 2048 : (g + 1) * 2048].rearrange("p (j m t) -> p t m j", j=4, m=P, t=4)
+            eng_copy(out=dst[:, t0:t1], in_=src[:, t0:t1])
+
+        def w1_quant(g):
+            nc.vector.quantize_mx(
+                out=w1c[:, g * F : (g + 1) * F].bitcast(FP8X4),
+                scales=w1s[:, g * F : (g + 1) * F],
+                in_=w1g[:, g * 2048 : (g + 1) * 2048],
+            )
+
+        w1_regroup(nc.vector.tensor_copy, 0, 0, 4)
+        nc.vector.quantize_mx(out=w2c[:].bitcast(FP8X4), scales=w2s[:], in_=w2g[:])
+        w1_regroup(nc.scalar.copy, 1, 2, 4)
+        w1_regroup(nc.vector.tensor_copy, 1, 0, 2)
+        w1_quant(0)
+        w1_quant(1)
+
+        res = keep.tile([P, J], F32, name="res")
+
+        st = {}
+
+        def transposes(s):
+            banks = []
+            for g in range(2):
+                for a in range(2):
+                    xt = psx.tile([P, 2, 256], F32, name="xt%d%d" % (g, a))
+                    xw = xin[(a, s)][:].bitcast(F32)
+                    for jj in range(2):
+                        for u in range(2):
+                            c0 = jj * 512 + (2 * g + u) * P
+                            nc.tensor.transpose(
+                                xt[:, u, jj * P : (jj + 1) * P], xw[:, c0 : c0 + P], ident[:]
+                            )
+                    banks.append(xt)
+            st[("xt", s)] = banks
+
+        def x_evac(s):
+            xg = work.tile([P, 2 * 2048], BF16, name="xg", align_bytes=64)
+            st[("xg", s)] = xg
+            view = xg[:].bitcast(F32).rearrange("p (g c u) -> p g c u", g=2, c=512, u=2)
+            k = 0
+            for g in range(2):
+                for a in range(2):
+                    dst = view[:, g, a * 256 : (a + 1) * 256, :]
+                    src = st[("xt", s)][k][:].rearrange("p u c -> p c u")
+                    if k < 3:
+                        nc.scalar.copy(out=dst, in_=src)
+                    else:
+                        nc.vector.tensor_copy(out=dst, in_=src)
+                    k += 1
+
+        def x_quant(s):
+            xc = work.tile([P, 2 * 512], U32, name="xc", align_bytes=64)
+            xs = work.tile([P, 2 * 512], U8, name="xs", align_bytes=64)
+            st[("xc", s)] = (xc, xs)
+            xg = st[("xg", s)]
+            for g in range(2):
+                nc.vector.quantize_mx(
+                    out=xc[:, g * 512 : (g + 1) * 512].bitcast(FP8X4),
+                    scales=xs[:, g * 512 : (g + 1) * 512],
+                    in_=xg[:, g * 2048 : (g + 1) * 2048],
+                )
+
+        def layer1(s):
+            xc, xs = st[("xc", s)]
+            hpl = work.tile([P, 4 * 512], BF16, name="hpl")
+            st[("hpl", s)] = hpl
+            for t in range(4):
+                hp = psh.tile([P, 512], F32, name="hp")
+                for g in range(2):
+                    w0 = g * F + t * P
+                    nc.tensor.matmul_mx(
+                        out=hp[:],
+                        lhsT=w1c[:, w0 : w0 + P].bitcast(FP8X4),
+                        lhsT_scale=w1s[:, w0 : w0 + P],
+                        rhs=xc[:, g * 512 : (g + 1) * 512].bitcast(FP8X4),
+                        rhs_scale=xs[:, g * 512 : (g + 1) * 512],
+                        start=(g == 0),
+                        stop=(g == 1),
+                    )
+                nc.scalar.activation(
+                    out=hpl[:, t * 512 : (t + 1) * 512],
+                    in_=hp[:],
+                    func=ACT.Relu,
+                    bias=b1f[:, t : t + 1],
+                    scale=1.0,
+                )
+
+        def h_regroup(s):
+            hg = work.tile([P, 2048], BF16, name="hg", align_bytes=64)
+            st[("hg", s)] = hg
+            nc.vector.tensor_copy(
+                out=hg[:].rearrange("p (c i t) -> p c t i", i=4, t=4),
+                in_=st[("hpl", s)][:].rearrange("p (t c i) -> p c t i", t=4, i=4),
+            )
+
+        def h_quant(s):
+            hc = work.tile([P, 512], U32, name="hc", align_bytes=64)
+            hs = work.tile([P, 512], U8, name="hs", align_bytes=64)
+            st[("hc", s)] = (hc, hs)
+            nc.vector.quantize_mx(out=hc[:].bitcast(FP8X4), scales=hs[:], in_=st[("hg", s)][:])
+
+        def layer2(s):
+            hc, hs = st[("hc", s)]
+            zp = psz.tile([P, 512], F32, name="zp")
+            st[("zp", s)] = zp
+            for b in range(4):
+                nc.tensor.matmul_mx(
+                    out=zp[:, b * P : (b + 1) * P],
+                    lhsT=hc[:, b * P : (b + 1) * P].bitcast(FP8X4),
+                    lhsT_scale=hs[:, b * P : (b + 1) * P],
+                    rhs=w2c[:].bitcast(FP8X4),
+                    rhs_scale=w2s[:],
+                    start=True,
+                    stop=True,
+                )
+
+        def z_diff(s):
+            m = work.tile([P, 512], F32, name="m")
+            nc.vector.tensor_tensor(
+                out=m[:].rearrange("p (b z) -> p b z", b=4),
+                in0=st[("zp", s)][:].rearrange("p (b z) -> p b z", b=4),
+                in1=negb2[:].unsqueeze(1).to_broadcast([P, 4, Z]),
+                op=ALU.max,
+            )
+            d = work.tile([P, 256], F32, name="d")
+            st[("d", s)] = d
+            nc.vector.tensor_tensor(out=d[:], in0=m[:, 0:256], in1=m[:, 256:512], op=ALU.subtract)
+
+        def z_square(s):
+            d = st[("d", s)]
+            for jj in range(2):
+                junk = work.tile([P, Z], F32, name="junk")
+                nc.scalar.activation(
+                    out=junk[:],
+                    in_=d[:, jj * Z : (jj + 1) * Z],
+                    func=ACT.Square,
+                    accum_out=res[:, 2 * s + jj : 2 * s + jj + 1],
+                )
+
+        def live(s):
+            return 0 <= s < ROUNDS
+
+        for s in range(-1, ROUNDS + 2):
+            if live(s - 2):
+                z_diff(s - 2)
+            if live(s - 1):
+                h_regroup(s - 1)
+            if live(s + 1):
+                transposes(s + 1)
+                x_evac(s + 1)
+            if live(s - 1):
+                h_quant(s - 1)
+            if live(s + 1):
+                x_quant(s + 1)
+            if live(s):
+                layer1(s)
+            if live(s - 1):
+                layer2(s - 1)
+            if live(s - 2):
+                z_square(s - 2)
+
+        o = keep.tile([P, J], F32, name="o")
+        nc.vector.scalar_tensor_tensor(
+            out=o[:], in0=res[:], scalar=1.0 / Z, in1=qf[:], op0=ALU.mult, op1=ALU.mult
+        )
+        nc.sync.dma_start(
+            out=out.rearrange("n m -> (n m)").rearrange("(p j) -> p j", j=J), in_=o[:]
+        )

@@ -20,6 +20,8 @@ J = ROWS // P
 ROUNDS = 16
 
 FLOPS = 2 * 2 * ROWS * (E * F + F * Z)
+LAG = 2
+DIFF_ON_GPSIMD = True
 
 
 def tile_querysiamese_pa_t_kernel(tc, xp1, xp2, W1, b1, W2, b2, q_energy, out):
@@ -109,35 +111,32 @@ def tile_querysiamese_pa_t_kernel(tc, xp1, xp2, W1, b1, W2, b2, q_energy, out):
 
         st = {}
 
-        def transposes(s):
-            banks = []
-            for g in range(2):
-                for a in range(2):
-                    xt = psx.tile([P, 2, 256], F32, name="xt%d%d" % (g, a))
-                    xw = xin[(a, s)][:].bitcast(F32)
-                    for jj in range(2):
-                        for u in range(2):
-                            c0 = jj * 512 + (2 * g + u) * P
-                            nc.tensor.transpose(
-                                xt[:, u, jj * P : (jj + 1) * P], xw[:, c0 : c0 + P], ident[:]
-                            )
-                    banks.append(xt)
-            st[("xt", s)] = banks
+        def transposes(s, ks):
+            for k in ks:
+                g, a = k // 2, k % 2
+                xt = psx.tile([P, 2, 256], F32, name="xt%d" % k)
+                xw = xin[(a, s)][:].bitcast(F32)
+                for jj in range(2):
+                    for u in range(2):
+                        c0 = jj * 512 + (2 * g + u) * P
+                        nc.tensor.transpose(
+                            xt[:, u, jj * P : (jj + 1) * P], xw[:, c0 : c0 + P], ident[:]
+                        )
+                st[("xt", s, k)] = xt
 
-        def x_evac(s):
-            xg = work.tile([P, 2 * 2048], BF16, name="xg", align_bytes=64)
-            st[("xg", s)] = xg
+        def x_evac(s, k, on_vector):
+            if ("xg", s) not in st:
+                xg_new = work.tile([P, 2 * 2048], BF16, name="xg", align_bytes=64)
+                st[("xg", s)] = xg_new
+            xg = st[("xg", s)]
+            g, a = k // 2, k % 2
             view = xg[:].bitcast(F32).rearrange("p (g c u) -> p g c u", g=2, c=512, u=2)
-            k = 0
-            for g in range(2):
-                for a in range(2):
-                    dst = view[:, g, a * 256 : (a + 1) * 256, :]
-                    src = st[("xt", s)][k][:].rearrange("p u c -> p c u")
-                    if k < 3:
-                        nc.scalar.copy(out=dst, in_=src)
-                    else:
-                        nc.vector.tensor_copy(out=dst, in_=src)
-                    k += 1
+            dst = view[:, g, a * 256 : (a + 1) * 256, :]
+            src = st[("xt", s, k)][:].rearrange("p u c -> p c u")
+            if on_vector:
+                nc.vector.tensor_copy(out=dst, in_=src)
+            else:
+                nc.scalar.copy(out=dst, in_=src)
 
         def x_quant(s):
             xc = work.tile([P, 2 * 512], U32, name="xc", align_bytes=64)
@@ -151,11 +150,13 @@ def tile_querysiamese_pa_t_kernel(tc, xp1, xp2, W1, b1, W2, b2, q_energy, out):
                     in_=xg[:, g * 2048 : (g + 1) * 2048],
                 )
 
-        def layer1(s):
+        def layer1(s, ts):
             xc, xs = st[("xc", s)]
-            hpl = work.tile([P, 4 * 512], BF16, name="hpl")
-            st[("hpl", s)] = hpl
-            for t in range(4):
+            if ("hpl", s) not in st:
+                hpl_new = work.tile([P, 4 * 512], BF16, name="hpl")
+                st[("hpl", s)] = hpl_new
+            hpl = st[("hpl", s)]
+            for t in ts:
                 hp = psh.tile([P, 512], F32, name="hp")
                 for g in range(2):
                     w0 = g * F + t * P
@@ -205,7 +206,7 @@ def tile_querysiamese_pa_t_kernel(tc, xp1, xp2, W1, b1, W2, b2, q_energy, out):
                     stop=True,
                 )
 
-        def z_diff(s):
+        def z_diff(s, diff_engine):
             m = work.tile([P, 512], F32, name="m")
             nc.vector.tensor_tensor(
                 out=m[:].rearrange("p (b z) -> p b z", b=4),
@@ -215,7 +216,7 @@ def tile_querysiamese_pa_t_kernel(tc, xp1, xp2, W1, b1, W2, b2, q_energy, out):
             )
             d = work.tile([P, 256], F32, name="d")
             st[("d", s)] = d
-            nc.vector.tensor_tensor(out=d[:], in0=m[:, 0:256], in1=m[:, 256:512], op=ALU.subtract)
+            diff_engine.tensor_tensor(out=d[:], in0=m[:, 0:256], in1=m[:, 256:512], op=ALU.subtract)
 
         def z_square(s):
             d = st[("d", s)]
@@ -231,24 +232,45 @@ def tile_querysiamese_pa_t_kernel(tc, xp1, xp2, W1, b1, W2, b2, q_energy, out):
         def live(s):
             return 0 <= s < ROUNDS
 
-        for s in range(-1, ROUNDS + 2):
-            if live(s - 2):
-                z_diff(s - 2)
+        def on_vector(s, k):
+            return k == 3 or (k == 1 and s % 2 == 0)
+
+        transposes(0, [0, 2, 1, 3])
+        x_evac(0, 0, False)
+        x_evac(0, 2, True)
+        x_evac(0, 1, False)
+        x_evac(0, 3, True)
+        x_quant(0)
+        transposes(1, [0, 2])
+        x_evac(1, 0, False)
+        x_evac(1, 2, False)
+        layer1(0, [0, 1])
+        transposes(1, [1, 3])
+        x_evac(1, 1, on_vector(1, 1))
+        x_evac(1, 3, on_vector(1, 3))
+        layer1(0, [2, 3])
+        x_quant(1)
+
+        for s in range(1, ROUNDS + LAG + 2):
+            zs = s - LAG - 1
+            if live(zs):
+                z_diff(zs, nc.gpsimd if (DIFF_ON_GPSIMD and zs < ROUNDS - 3) else nc.vector)
             if live(s - 1):
                 h_regroup(s - 1)
             if live(s + 1):
-                transposes(s + 1)
-                x_evac(s + 1)
+                transposes(s + 1, [0, 1, 2, 3])
+                for k in range(4):
+                    x_evac(s + 1, k, on_vector(s + 1, k))
             if live(s - 1):
                 h_quant(s - 1)
             if live(s + 1):
                 x_quant(s + 1)
             if live(s):
-                layer1(s)
-            if live(s - 1):
-                layer2(s - 1)
-            if live(s - 2):
-                z_square(s - 2)
+                layer1(s, [0, 1, 2, 3])
+            if live(s - LAG):
+                layer2(s - LAG)
+            if live(zs):
+                z_square(zs)
 
         o = keep.tile([P, J], F32, name="o")
         nc.vector.scalar_tensor_tensor(

@@ -233,7 +233,7 @@ def tile_querysiamese_pa_t_kernel(tc, xp1, xp2, W1, b1, W2, b2, q_energy, out):
             return 0 <= s < ROUNDS
 
         def on_vector(s, k):
-            return k == 3 or (k == 1 and s % 2 == 0)
+            return k == 3 or k == 1
 
         transposes(0, [0, 2, 1, 3])
         x_evac(0, 0, False)

@@ -143,12 +143,7 @@ def tile_querysiamese_pa_t_kernel(tc, xp1, xp2, W1, b1, W2, b2, q_energy, out):
             xs = work.tile([P, 2 * 512], U8, name="xs", align_bytes=64)
             st[("xc", s)] = (xc, xs)
             xg = st[("xg", s)]
-            for g in range(2):
-                nc.vector.quantize_mx(
-                    out=xc[:, g * 512 : (g + 1) * 512].bitcast(FP8X4),
-                    scales=xs[:, g * 512 : (g + 1) * 512],
-                    in_=xg[:, g * 2048 : (g + 1) * 2048],
-                )
+            nc.vector.quantize_mx(out=xc[:].bitcast(FP8X4), scales=xs[:], in_=xg[:])
 
         def layer1(s, ts):
             xc, xs = st[("xc", s)]
@@ -233,7 +228,7 @@ def tile_querysiamese_pa_t_kernel(tc, xp1, xp2, W1, b1, W2, b2, q_energy, out):
             return 0 <= s < ROUNDS
 
         def on_vector(s, k):
-            return k == 3 or k == 1
+            return k == 3
 
         transposes(0, [0, 2, 1, 3])
         x_evac(0, 0, False)
@@ -241,15 +236,13 @@ def tile_querysiamese_pa_t_kernel(tc, xp1, xp2, W1, b1, W2, b2, q_energy, out):
         x_evac(0, 1, False)
         x_evac(0, 3, True)
         x_quant(0)
-        transposes(1, [0, 2])
+        transposes(1, [0, 2, 1, 3])
         x_evac(1, 0, False)
         x_evac(1, 2, False)
-        layer1(0, [0, 1])
-        transposes(1, [1, 3])
-        x_evac(1, 1, on_vector(1, 1))
-        x_evac(1, 3, on_vector(1, 3))
-        layer1(0, [2, 3])
+        x_evac(1, 1, False)
+        x_evac(1, 3, True)
         x_quant(1)
+        layer1(0, [0, 1, 2, 3])
 
         for s in range(1, ROUNDS + LAG + 2):
             zs = s - LAG - 1

@@ -17,11 +17,13 @@ F = 512
 Z = 128
 ROWS = 4096
 J = ROWS // P
-ROUNDS = 16
+
+WIDTHS = [1, 1] + [2] * 14 + [1, 1]
+STARTS = [sum(WIDTHS[:s]) for s in range(len(WIDTHS))]
+ROUNDS = len(WIDTHS)
 
 FLOPS = 2 * 2 * ROWS * (E * F + F * Z)
 LAG = 2
-DIFF_ON_GPSIMD = True
 
 
 def tile_querysiamese_pa_t_kernel(tc, xp1, xp2, W1, b1, W2, b2, q_energy, out):
@@ -52,41 +54,38 @@ def tile_querysiamese_pa_t_kernel(tc, xp1, xp2, W1, b1, W2, b2, q_energy, out):
 
         w1v = W1.rearrange("(c p e) f -> p c (e f)", c=4, p=P, e=2)
         w1r = keep.tile([P, 8 * F], BF16, name="w1r")
+        xin = {}
+
+        def load_x(s):
+            nj, j0 = WIDTHS[s], STARTS[s]
+            for a in range(2):
+                xt_in = keep.tile([P, nj * E], BF16, name="x%d_%d" % (a, s))
+                nc.sync.dma_start(
+                    out=xt_in[:].rearrange("p (j k) -> p j k", j=nj),
+                    in_=xv[a][:, j0 : j0 + nj, :],
+                )
+                xin[(a, s)] = xt_in
+
+        load_x(0)
         for g in range(2):
             nc.sync.dma_start(
                 out=w1r[:, g * 2048 : (g + 1) * 2048].rearrange("p (u x) -> p u x", u=2),
                 in_=w1v[:, 2 * g : 2 * g + 2, :],
             )
-        xin = {}
-        for s in range(ROUNDS):
-            for a in range(2):
-                xt_in = keep.tile([P, 2 * E], BF16, name="x%d_%d" % (a, s))
-                nc.sync.dma_start(
-                    out=xt_in[:].rearrange("p (j k) -> p j k", j=2),
-                    in_=xv[a][:, 2 * s : 2 * s + 2, :],
-                )
-                xin[(a, s)] = xt_in
+        for s in range(1, ROUNDS):
+            load_x(s)
 
         ident = keep.tile([P, P], F32, name="ident")
         make_identity(nc, ident[:])
 
-        b1f = keep.tile([P, 4], F32, name="b1f")
-        nc.vector.tensor_copy(out=b1f[:], in_=b1r[:])
         negb2 = keep.tile([P, Z], F32, name="negb2")
-        nc.vector.tensor_scalar(out=negb2[:], in0=b2r[:], scalar1=-1.0, scalar2=None, op0=ALU.mult)
-        qf = keep.tile([P, J], F32, name="qf")
-        nc.vector.tensor_copy(out=qf[:], in_=qr[:])
         w2g = keep.tile([P, 4 * Z], BF16, name="w2g", align_bytes=64)
-        nc.vector.tensor_copy(
-            out=w2g[:].rearrange("p (z t) -> p z t", t=4),
-            in_=w2r[:].rearrange("p (t z) -> p z t", t=4),
-        )
         w2c = keep.tile([P, Z], U32, name="w2c", align_bytes=64)
         w2s = keep.tile([P, Z], U8, name="w2s", align_bytes=64)
-
         w1g = keep.tile([P, 8 * F], BF16, name="w1g", align_bytes=64)
         w1c = keep.tile([P, 2 * F], U32, name="w1c", align_bytes=64)
         w1s = keep.tile([P, 2 * F], U8, name="w1s", align_bytes=64)
+        res = keep.tile([P, J], F32, name="res")
 
         def w1_regroup(eng_copy, g, t0, t1):
             dst = w1g[:, g * 2048 : (g + 1) * 2048].rearrange("p (t m j) -> p t m j", t=4, m=P, j=4)
@@ -100,97 +99,109 @@ def tile_querysiamese_pa_t_kernel(tc, xp1, xp2, W1, b1, W2, b2, q_energy, out):
                 in_=w1g[:, g * 2048 : (g + 1) * 2048],
             )
 
-        w1_regroup(nc.vector.tensor_copy, 0, 0, 4)
-        nc.vector.quantize_mx(out=w2c[:].bitcast(FP8X4), scales=w2s[:], in_=w2g[:])
-        w1_regroup(nc.scalar.copy, 1, 2, 4)
-        w1_regroup(nc.vector.tensor_copy, 1, 0, 2)
-        w1_quant(0)
-        w1_quant(1)
-
-        res = keep.tile([P, J], F32, name="res")
+        def layer2_constants():
+            nc.vector.tensor_copy(
+                out=w2g[:].rearrange("p (z t) -> p z t", t=4),
+                in_=w2r[:].rearrange("p (t z) -> p z t", t=4),
+            )
+            nc.vector.tensor_scalar(
+                out=negb2[:], in0=b2r[:], scalar1=-1.0, scalar2=None, op0=ALU.mult
+            )
+            nc.vector.quantize_mx(out=w2c[:].bitcast(FP8X4), scales=w2s[:], in_=w2g[:])
 
         st = {}
 
-        def transposes(s, ks):
-            for k in ks:
-                g, a = k // 2, k % 2
+        def banks(s):
+            if WIDTHS[s] == 2:
+                return [(0, 0, 0, 0), (1, 0, 1, 256), (2, 1, 0, 0), (3, 1, 1, 256)]
+            return [(0, 0, None, 0), (1, 1, None, 0)]
+
+        def transposes(s):
+            for k, g, tower, _ in banks(s):
                 xt = psx.tile([P, 2, 256], F32, name="xt%d" % k)
-                xw = xin[(a, s)][:].bitcast(F32)
-                for jj in range(2):
+                halves = [(tower, 0), (tower, 1)] if tower is not None else [(0, 0), (1, 0)]
+                for h, (a, jj) in enumerate(halves):
+                    xw = xin[(a, s)][:].bitcast(F32)
                     for u in range(2):
                         c0 = jj * 512 + (2 * g + u) * P
                         nc.tensor.transpose(
-                            xt[:, u, jj * P : (jj + 1) * P], xw[:, c0 : c0 + P], ident[:]
+                            xt[:, u, h * P : (h + 1) * P], xw[:, c0 : c0 + P], ident[:]
                         )
                 st[("xt", s, k)] = xt
 
-        def x_evac(s, k, on_vector):
-            if ("xg", s) not in st:
-                xg_new = work.tile([P, 2 * 2048], BF16, name="xg", align_bytes=64)
-                st[("xg", s)] = xg_new
-            xg = st[("xg", s)]
-            g, a = k // 2, k % 2
-            view = xg[:].bitcast(F32).rearrange("p (g c u) -> p g c u", g=2, c=512, u=2)
-            dst = view[:, g, a * 256 : (a + 1) * 256, :]
-            src = st[("xt", s, k)][:].rearrange("p u c -> p c u")
-            if on_vector:
-                nc.vector.tensor_copy(out=dst, in_=src)
-            else:
-                nc.scalar.copy(out=dst, in_=src)
+        def x_evac(s, copies):
+            cols = 256 * WIDTHS[s]
+            xg = work.tile([P, 2 * 2048], BF16, name="xg", align_bytes=64)
+            st[("xg", s)] = xg
+            view = xg[:, 0 : 8 * cols].bitcast(F32).rearrange("p (g c u) -> p g c u", g=2, c=cols, u=2)
+            for (k, g, _, c0), eng_copy in zip(banks(s), copies):
+                eng_copy(
+                    out=view[:, g, c0 : c0 + 256, :],
+                    in_=st[("xt", s, k)][:].rearrange("p u c -> p c u"),
+                )
 
         def x_quant(s):
+            cols = 256 * WIDTHS[s]
             xc = work.tile([P, 2 * 512], U32, name="xc", align_bytes=64)
             xs = work.tile([P, 2 * 512], U8, name="xs", align_bytes=64)
             st[("xc", s)] = (xc, xs)
-            xg = st[("xg", s)]
-            nc.vector.quantize_mx(out=xc[:].bitcast(FP8X4), scales=xs[:], in_=xg[:])
+            nc.vector.quantize_mx(
+                out=xc[:, 0 : 2 * cols].bitcast(FP8X4),
+                scales=xs[:, 0 : 2 * cols],
+                in_=st[("xg", s)][:, 0 : 8 * cols],
+            )
 
-        def layer1(s, ts):
+        def layer1(s):
+            cols = 256 * WIDTHS[s]
             xc, xs = st[("xc", s)]
-            if ("hpl", s) not in st:
-                hpl_new = work.tile([P, 4 * 512], BF16, name="hpl")
-                st[("hpl", s)] = hpl_new
-            hpl = st[("hpl", s)]
-            for t in ts:
+            hpl = work.tile([P, 4 * 512], BF16, name="hpl")
+            st[("hpl", s)] = hpl
+            for t in range(4):
                 hp = psh.tile([P, 512], F32, name="hp")
                 for g in range(2):
                     w0 = g * F + t * P
                     nc.tensor.matmul_mx(
-                        out=hp[:],
+                        out=hp[:, 0:cols],
                         lhsT=w1c[:, w0 : w0 + P].bitcast(FP8X4),
                         lhsT_scale=w1s[:, w0 : w0 + P],
-                        rhs=xc[:, g * 512 : (g + 1) * 512].bitcast(FP8X4),
-                        rhs_scale=xs[:, g * 512 : (g + 1) * 512],
+                        rhs=xc[:, g * cols : (g + 1) * cols].bitcast(FP8X4),
+                        rhs_scale=xs[:, g * cols : (g + 1) * cols],
                         start=(g == 0),
                         stop=(g == 1),
                     )
                 nc.scalar.activation(
-                    out=hpl[:, t * 512 : (t + 1) * 512],
-                    in_=hp[:],
+                    out=hpl[:, t * cols : (t + 1) * cols],
+                    in_=hp[:, 0:cols],
                     func=ACT.Relu,
-                    bias=b1f[:, t : t + 1],
+                    bias=b1r[:, t : t + 1],
                     scale=1.0,
                 )
 
         def h_regroup(s):
+            cols = 256 * WIDTHS[s]
             hg = work.tile([P, 2048], BF16, name="hg", align_bytes=64)
             st[("hg", s)] = hg
             nc.vector.tensor_copy(
-                out=hg[:].rearrange("p (c i t) -> p c t i", i=4, t=4),
-                in_=st[("hpl", s)][:].rearrange("p (t c i) -> p c t i", t=4, i=4),
+                out=hg[:, 0 : 4 * cols].rearrange("p (c i t) -> p c t i", i=4, t=4),
+                in_=st[("hpl", s)][:, 0 : 4 * cols].rearrange("p (t c i) -> p c t i", t=4, i=4),
             )
 
         def h_quant(s):
+            cols = 256 * WIDTHS[s]
             hc = work.tile([P, 512], U32, name="hc", align_bytes=64)
             hs = work.tile([P, 512], U8, name="hs", align_bytes=64)
             st[("hc", s)] = (hc, hs)
-            nc.vector.quantize_mx(out=hc[:].bitcast(FP8X4), scales=hs[:], in_=st[("hg", s)][:])
+            nc.vector.quantize_mx(
+                out=hc[:, 0:cols].bitcast(FP8X4),
+                scales=hs[:, 0:cols],
+                in_=st[("hg", s)][:, 0 : 4 * cols],
+            )
 
         def layer2(s):
             hc, hs = st[("hc", s)]
             zp = psz.tile([P, 512], F32, name="zp")
             st[("zp", s)] = zp
-            for b in range(4):
+            for b in range(2 * WIDTHS[s]):
                 nc.tensor.matmul_mx(
                     out=zp[:, b * P : (b + 1) * P],
                     lhsT=hc[:, b * P : (b + 1) * P].bitcast(FP8X4),
@@ -202,64 +213,68 @@ def tile_querysiamese_pa_t_kernel(tc, xp1, xp2, W1, b1, W2, b2, q_energy, out):
                 )
 
         def z_diff(s, diff_engine):
+            blocks = 2 * WIDTHS[s]
+            half = WIDTHS[s] * P
             m = work.tile([P, 512], F32, name="m")
             nc.vector.tensor_tensor(
-                out=m[:].rearrange("p (b z) -> p b z", b=4),
-                in0=st[("zp", s)][:].rearrange("p (b z) -> p b z", b=4),
-                in1=negb2[:].unsqueeze(1).to_broadcast([P, 4, Z]),
+                out=m[:, 0 : 2 * half].rearrange("p (b z) -> p b z", b=blocks),
+                in0=st[("zp", s)][:, 0 : 2 * half].rearrange("p (b z) -> p b z", b=blocks),
+                in1=negb2[:].unsqueeze(1).to_broadcast([P, blocks, Z]),
                 op=ALU.max,
             )
             d = work.tile([P, 256], F32, name="d")
             st[("d", s)] = d
-            diff_engine.tensor_tensor(out=d[:], in0=m[:, 0:256], in1=m[:, 256:512], op=ALU.subtract)
+            diff_engine.tensor_tensor(
+                out=d[:, 0:half], in0=m[:, 0:half], in1=m[:, half : 2 * half], op=ALU.subtract
+            )
 
         def z_square(s):
             d = st[("d", s)]
-            for jj in range(2):
+            for jj in range(WIDTHS[s]):
                 junk = work.tile([P, Z], F32, name="junk")
+                c = STARTS[s] + jj
                 nc.scalar.activation(
                     out=junk[:],
                     in_=d[:, jj * Z : (jj + 1) * Z],
                     func=ACT.Square,
-                    accum_out=res[:, 2 * s + jj : 2 * s + jj + 1],
+                    accum_out=res[:, c : c + 1],
                 )
 
         def live(s):
             return 0 <= s < ROUNDS
 
-        def on_vector(s, k):
-            return k == 3
+        vcopy, scopy = nc.vector.tensor_copy, nc.scalar.copy
 
-        transposes(0, [0, 2, 1, 3])
-        x_evac(0, 0, False)
-        x_evac(0, 2, True)
-        x_evac(0, 1, False)
-        x_evac(0, 3, True)
+        def evac_engines(s):
+            return [scopy, scopy, scopy, vcopy] if WIDTHS[s] == 2 else [scopy, vcopy]
+
+        transposes(0)
+        x_evac(0, evac_engines(0))
         x_quant(0)
-        transposes(1, [0, 2, 1, 3])
-        x_evac(1, 0, False)
-        x_evac(1, 2, False)
-        x_evac(1, 1, False)
-        x_evac(1, 3, True)
-        x_quant(1)
-        layer1(0, [0, 1, 2, 3])
+        w1_regroup(scopy, 0, 2, 4)
+        w1_regroup(vcopy, 0, 0, 2)
+        w1_quant(0)
+        w1_regroup(scopy, 1, 2, 4)
+        w1_regroup(vcopy, 1, 0, 2)
+        w1_quant(1)
 
-        for s in range(1, ROUNDS + LAG + 2):
+        for s in range(ROUNDS + LAG + 1):
             zs = s - LAG - 1
+            if s == 1:
+                layer2_constants()
             if live(zs):
-                z_diff(zs, nc.gpsimd if (DIFF_ON_GPSIMD and zs < ROUNDS - 3) else nc.vector)
+                z_diff(zs, nc.gpsimd if zs < ROUNDS - 4 else nc.vector)
             if live(s - 1):
                 h_regroup(s - 1)
             if live(s + 1):
-                transposes(s + 1, [0, 1, 2, 3])
-                for k in range(4):
-                    x_evac(s + 1, k, on_vector(s + 1, k))
+                transposes(s + 1)
+                x_evac(s + 1, evac_engines(s + 1))
             if live(s - 1):
                 h_quant(s - 1)
             if live(s + 1):
                 x_quant(s + 1)
             if live(s):
-                layer1(s, [0, 1, 2, 3])
+                layer1(s)
             if live(s - LAG):
                 layer2(s - LAG)
             if live(zs):
@@ -267,7 +282,7 @@ def tile_querysiamese_pa_t_kernel(tc, xp1, xp2, W1, b1, W2, b2, q_energy, out):
 
         o = keep.tile([P, J], F32, name="o")
         nc.vector.scalar_tensor_tensor(
-            out=o[:], in0=res[:], scalar=1.0 / Z, in1=qf[:], op0=ALU.mult, op1=ALU.mult
+            out=o[:], in0=res[:], scalar=1.0 / Z, in1=qr[:], op0=ALU.mult, op1=ALU.mult
         )
         nc.sync.dma_start(
             out=out.rearrange("n m -> (n m)").rearrange("(p j) -> p j", j=J), in_=o[:]

@@ -41,16 +41,18 @@ def tile_querysiamese_pa_t_kernel(tc, xp1, xp2, W1, b1, W2, b2, q_energy, out):
             for xp in (xp1, xp2)
         ]
 
+        ident = keep.tile([P, P], F32, name="ident")
+        make_identity(nc, ident[:])
+
         b1r = keep.tile([P, 4], BF16, name="b1r")
         nc.scalar.dma_start(out=b1r[:], in_=b1.rearrange("(p t) -> p t", t=4))
+
+        ones = keep.tile([P, P], BF16, name="ones")
+        nc.gpsimd.memset(ones[:], 1.0)
+        b2row = keep.tile([P, Z], BF16, name="b2row")
+        nc.gpsimd.memset(b2row[:], 0.0)
         w2r = keep.tile([P, 4 * Z], BF16, name="w2r")
-        nc.scalar.dma_start(out=w2r[:], in_=W2.rearrange("(p t) z -> p (t z)", t=4))
-        b2r = keep.tile([P, Z], BF16, name="b2r")
-        nc.scalar.dma_start(out=b2r[:], in_=b2.partition_broadcast(P))
         qr = keep.tile([P, J], BF16, name="qr")
-        nc.scalar.dma_start(
-            out=qr[:], in_=q_energy.rearrange("n m -> (n m)").rearrange("(p j) -> p j", j=J)
-        )
 
         w1v = W1.rearrange("(c p e) f -> p c (e f)", c=4, p=P, e=2)
         w1r = keep.tile([P, 8 * F], BF16, name="w1r")
@@ -66,17 +68,23 @@ def tile_querysiamese_pa_t_kernel(tc, xp1, xp2, W1, b1, W2, b2, q_energy, out):
                 )
                 xin[(a, s)] = xt_in
 
-        load_x(0)
-        for g in range(2):
+        def load_w1(g):
             nc.sync.dma_start(
                 out=w1r[:, g * 2048 : (g + 1) * 2048].rearrange("p (u x) -> p u x", u=2),
                 in_=w1v[:, 2 * g : 2 * g + 2, :],
             )
-        for s in range(1, ROUNDS):
-            load_x(s)
 
-        ident = keep.tile([P, P], F32, name="ident")
-        make_identity(nc, ident[:])
+        load_w1(0)
+        load_x(0)
+        load_w1(1)
+        load_x(1)
+        nc.sync.dma_start(out=w2r[:], in_=W2.rearrange("(p t) z -> p (t z)", t=4))
+        nc.sync.dma_start(out=b2row[0:1, :], in_=b2.rearrange("(o z) -> o z", o=1))
+        for s in range(2, ROUNDS):
+            load_x(s)
+        nc.sync.dma_start(
+            out=qr[:], in_=q_energy.rearrange("n m -> (n m)").rearrange("(p j) -> p j", j=J)
+        )
 
         negb2 = keep.tile([P, Z], F32, name="negb2")
         w2g = keep.tile([P, 4 * Z], BF16, name="w2g", align_bytes=64)
@@ -104,8 +112,10 @@ def tile_querysiamese_pa_t_kernel(tc, xp1, xp2, W1, b1, W2, b2, q_energy, out):
                 out=w2g[:].rearrange("p (z t) -> p z t", t=4),
                 in_=w2r[:].rearrange("p (t z) -> p z t", t=4),
             )
+            b2p = psz.tile([P, 512], F32, name="zp")
+            nc.tensor.matmul(b2p[:, 0:Z], lhsT=ones[:], rhs=b2row[:], start=True, stop=True)
             nc.vector.tensor_scalar(
-                out=negb2[:], in0=b2r[:], scalar1=-1.0, scalar2=None, op0=ALU.mult
+                out=negb2[:], in0=b2p[:, 0:Z], scalar1=-1.0, scalar2=None, op0=ALU.mult
             )
             nc.vector.quantize_mx(out=w2c[:].bitcast(FP8X4), scales=w2s[:], in_=w2g[:])
 
@@ -248,12 +258,12 @@ def tile_querysiamese_pa_t_kernel(tc, xp1, xp2, W1, b1, W2, b2, q_energy, out):
         def evac_engines(s):
             return [scopy, scopy, scopy, vcopy] if WIDTHS[s] == 2 else [scopy, vcopy]
 
+        w1_regroup(scopy, 0, 3, 4)
+        w1_regroup(vcopy, 0, 0, 3)
+        w1_quant(0)
         transposes(0)
         x_evac(0, evac_engines(0))
         x_quant(0)
-        w1_regroup(scopy, 0, 2, 4)
-        w1_regroup(vcopy, 0, 0, 2)
-        w1_quant(0)
         w1_regroup(scopy, 1, 2, 4)
         w1_regroup(vcopy, 1, 0, 2)
         w1_quant(1)

@@ -18,7 +18,7 @@ Z = 128
 ROWS = 4096
 J = ROWS // P
 
-WIDTHS = [1, 1] + [2] * 14 + [1, 1]
+WIDTHS = [1] + [2] * 15 + [1]
 STARTS = [sum(WIDTHS[:s]) for s in range(len(WIDTHS))]
 ROUNDS = len(WIDTHS)
 
@@ -191,10 +191,12 @@ def tile_querysiamese_pa_t_kernel(tc, xp1, xp2, W1, b1, W2, b2, q_energy, out):
             cols = 256 * WIDTHS[s]
             hg = work.tile([P, 2048], BF16, name="hg", align_bytes=64)
             st[("hg", s)] = hg
-            nc.vector.tensor_copy(
-                out=hg[:, 0 : 4 * cols].rearrange("p (c i t) -> p c t i", i=4, t=4),
-                in_=st[("hpl", s)][:, 0 : 4 * cols].rearrange("p (t c i) -> p c t i", t=4, i=4),
-            )
+            dst = hg[:, 0 : 4 * cols].rearrange("p (c i t) -> p c t i", i=4, t=4)
+            src = st[("hpl", s)][:, 0 : 4 * cols].rearrange("p (t c i) -> p c t i", t=4, i=4)
+            cut = cols // 4 if s < ROUNDS - 1 else cols // 8
+            if cut < cols // 4:
+                nc.scalar.copy(out=dst[:, cut:], in_=src[:, cut:])
+            nc.vector.tensor_copy(out=dst[:, 0:cut], in_=src[:, 0:cut])
 
         def h_quant(s):
             cols = 256 * WIDTHS[s]
@@ -256,10 +258,11 @@ def tile_querysiamese_pa_t_kernel(tc, xp1, xp2, W1, b1, W2, b2, q_energy, out):
         vcopy, scopy = nc.vector.tensor_copy, nc.scalar.copy
 
         def evac_engines(s):
-            return [scopy, scopy, scopy, vcopy] if WIDTHS[s] == 2 else [scopy, vcopy]
+            if WIDTHS[s] == 2:
+                return [scopy, scopy, scopy, vcopy]
+            return [scopy, vcopy] if s == 0 else [scopy, scopy]
 
-        w1_regroup(scopy, 0, 3, 4)
-        w1_regroup(vcopy, 0, 0, 3)
+        w1_regroup(vcopy, 0, 0, 4)
         w1_quant(0)
         transposes(0)
         x_evac(0, evac_engines(0))
@@ -273,7 +276,7 @@ def tile_querysiamese_pa_t_kernel(tc, xp1, xp2, W1, b1, W2, b2, q_energy, out):
             if s == 1:
                 layer2_constants()
             if live(zs):
-                z_diff(zs, nc.gpsimd if zs < ROUNDS - 4 else nc.vector)
+                z_diff(zs, nc.gpsimd if zs < ROUNDS - 2 else nc.vector)
             if live(s - 1):
                 h_regroup(s - 1)
             if live(s + 1):

@@ -32,8 +32,7 @@ def tile_querysiamese_pa_t_kernel(tc, xp1, xp2, W1, b1, W2, b2, q_energy, out):
         keep = ctx.enter_context(tc.tile_pool(name="keep", bufs=1))
         work = ctx.enter_context(tc.tile_pool(name="work", bufs=2))
         psx = ctx.enter_context(tc.psum_pool(name="psx", bufs=1))
-        psh = ctx.enter_context(tc.psum_pool(name="psh", bufs=3))
-        psz = ctx.enter_context(tc.psum_pool(name="psz", bufs=1))
+        psh = ctx.enter_context(tc.psum_pool(name="psh", bufs=4))
         ctx.enter_context(tc.manual_schedule())
 
         xv = [
@@ -112,7 +111,7 @@ def tile_querysiamese_pa_t_kernel(tc, xp1, xp2, W1, b1, W2, b2, q_energy, out):
                 out=w2g[:].rearrange("p (z t) -> p z t", t=4),
                 in_=w2r[:].rearrange("p (t z) -> p z t", t=4),
             )
-            b2p = psz.tile([P, 512], F32, name="zp")
+            b2p = psh.tile([P, 512], F32, name="hp")
             nc.tensor.matmul(b2p[:, 0:Z], lhsT=ones[:], rhs=b2row[:], start=True, stop=True)
             nc.vector.tensor_scalar(
                 out=negb2[:], in0=b2p[:, 0:Z], scalar1=-1.0, scalar2=None, op0=ALU.mult
@@ -211,7 +210,7 @@ def tile_querysiamese_pa_t_kernel(tc, xp1, xp2, W1, b1, W2, b2, q_energy, out):
 
         def layer2(s):
             hc, hs = st[("hc", s)]
-            zp = psz.tile([P, 512], F32, name="zp")
+            zp = psh.tile([P, 512], F32, name="hp")
             st[("zp", s)] = zp
             for b in range(2 * WIDTHS[s]):
                 nc.tensor.matmul_mx(
@@ -258,6 +257,8 @@ def tile_querysiamese_pa_t_kernel(tc, xp1, xp2, W1, b1, W2, b2, q_energy, out):
         vcopy, scopy = nc.vector.tensor_copy, nc.scalar.copy
 
         def evac_engines(s):
+            if s == 1:
+                return [scopy, vcopy, scopy, vcopy]
             if WIDTHS[s] == 2:
                 return [scopy, scopy, scopy, vcopy]
             return [scopy, vcopy] if s == 0 else [scopy, scopy]

@@ -31,8 +31,7 @@ def tile_querysiamese_pa_t_kernel(tc, xp1, xp2, W1, b1, W2, b2, q_energy, out):
     with ExitStack() as ctx:
         keep = ctx.enter_context(tc.tile_pool(name="keep", bufs=1))
         work = ctx.enter_context(tc.tile_pool(name="work", bufs=2))
-        psx = ctx.enter_context(tc.psum_pool(name="psx", bufs=1))
-        psh = ctx.enter_context(tc.psum_pool(name="psh", bufs=4))
+        ps = ctx.enter_context(tc.psum_pool(name="ps", bufs=8))
         ctx.enter_context(tc.manual_schedule())
 
         xv = [
@@ -111,7 +110,7 @@ def tile_querysiamese_pa_t_kernel(tc, xp1, xp2, W1, b1, W2, b2, q_energy, out):
                 out=w2g[:].rearrange("p (z t) -> p z t", t=4),
                 in_=w2r[:].rearrange("p (t z) -> p z t", t=4),
             )
-            b2p = psh.tile([P, 512], F32, name="hp")
+            b2p = ps.tile([P, 512], F32, name="bank")
             nc.tensor.matmul(b2p[:, 0:Z], lhsT=ones[:], rhs=b2row[:], start=True, stop=True)
             nc.vector.tensor_scalar(
                 out=negb2[:], in0=b2p[:, 0:Z], scalar1=-1.0, scalar2=None, op0=ALU.mult
@@ -122,12 +121,12 @@ def tile_querysiamese_pa_t_kernel(tc, xp1, xp2, W1, b1, W2, b2, q_energy, out):
 
         def banks(s):
             if WIDTHS[s] == 2:
-                return [(0, 0, 0, 0), (1, 0, 1, 256), (2, 1, 0, 0), (3, 1, 1, 256)]
+                return [(0, 0, 0, 0), (1, 1, 0, 0), (2, 0, 1, 256), (3, 1, 1, 256)]
             return [(0, 0, None, 0), (1, 1, None, 0)]
 
         def transposes(s):
             for k, g, tower, _ in banks(s):
-                xt = psx.tile([P, 2, 256], F32, name="xt%d" % k)
+                xt = ps.tile([P, 2, 256], F32, name="bank")
                 halves = [(tower, 0), (tower, 1)] if tower is not None else [(0, 0), (1, 0)]
                 for h, (a, jj) in enumerate(halves):
                     xw = xin[(a, s)][:].bitcast(F32)
@@ -166,7 +165,7 @@ def tile_querysiamese_pa_t_kernel(tc, xp1, xp2, W1, b1, W2, b2, q_energy, out):
             hpl = work.tile([P, 4 * 512], BF16, name="hpl")
             st[("hpl", s)] = hpl
             for t in range(4):
-                hp = psh.tile([P, 512], F32, name="hp")
+                hp = ps.tile([P, 512], F32, name="bank")
                 for g in range(2):
                     w0 = g * F + t * P
                     nc.tensor.matmul_mx(
@@ -178,13 +177,19 @@ def tile_querysiamese_pa_t_kernel(tc, xp1, xp2, W1, b1, W2, b2, q_energy, out):
                         start=(g == 0),
                         stop=(g == 1),
                     )
-                nc.scalar.activation(
-                    out=hpl[:, t * cols : (t + 1) * cols],
-                    in_=hp[:, 0:cols],
-                    func=ACT.Relu,
-                    bias=b1r[:, t : t + 1],
-                    scale=1.0,
-                )
+                if t == 0 and WIDTHS[s] == 2:
+                    nc.vector.tensor_scalar(
+                        out=hpl[:, 0:cols], in0=hp[:, 0:cols],
+                        scalar1=b1f[:, 0:1], scalar2=0.0, op0=ALU.add, op1=ALU.max,
+                    )
+                else:
+                    nc.scalar.activation(
+                        out=hpl[:, t * cols : (t + 1) * cols],
+                        in_=hp[:, 0:cols],
+                        func=ACT.Relu,
+                        bias=b1r[:, t : t + 1],
+                        scale=1.0,
+                    )
 
         def h_regroup(s):
             cols = 256 * WIDTHS[s]
@@ -210,7 +215,7 @@ def tile_querysiamese_pa_t_kernel(tc, xp1, xp2, W1, b1, W2, b2, q_energy, out):
 
         def layer2(s):
             hc, hs = st[("hc", s)]
-            zp = psh.tile([P, 512], F32, name="hp")
+            zp = ps.tile([P, 512], F32, name="bank")
             st[("zp", s)] = zp
             for b in range(2 * WIDTHS[s]):
                 nc.tensor.matmul_mx(
@@ -260,8 +265,11 @@ def tile_querysiamese_pa_t_kernel(tc, xp1, xp2, W1, b1, W2, b2, q_energy, out):
             if s == 1:
                 return [scopy, vcopy, scopy, vcopy]
             if WIDTHS[s] == 2:
-                return [scopy, scopy, scopy, vcopy]
+                return [scopy, scopy, scopy, scopy]
             return [scopy, vcopy] if s == 0 else [scopy, scopy]
+
+        b1f = keep.tile([P, 4], F32, name="b1f")
+        nc.vector.tensor_copy(out=b1f[:], in_=b1r[:])
 
         w1_regroup(vcopy, 0, 0, 4)
         w1_quant(0)
@@ -283,12 +291,12 @@ def tile_querysiamese_pa_t_kernel(tc, xp1, xp2, W1, b1, W2, b2, q_energy, out):
             if live(s + 1):
                 transposes(s + 1)
                 x_evac(s + 1, evac_engines(s + 1))
+            if live(s):
+                layer1(s)
             if live(s - 1):
                 h_quant(s - 1)
             if live(s + 1):
                 x_quant(s + 1)
-            if live(s):
-                layer1(s)
             if live(s - LAG):
                 layer2(s - LAG)
             if live(zs):

from contextlib import ExitStack

import concourse.mybir as mybir
from concourse.masks import make_identity

F32 = mybir.dt.float32
BF16 = mybir.dt.bfloat16
U32 = mybir.dt.uint32
U8 = mybir.dt.uint8
FP8X4 = mybir.dt.float8_e4m3fn_x4
ACT = mybir.ActivationFunctionType
ALU = mybir.AluOpType

P = 128
E = 1024
F = 512
Z = 128
ROWS = 4096
J = ROWS // P

WIDTHS = [1] + [2] * 15 + [1]
STARTS = [sum(WIDTHS[:s]) for s in range(len(WIDTHS))]
ROUNDS = len(WIDTHS)

FLOPS = 2 * 2 * ROWS * (E * F + F * Z)
LAG = 2


def tile_querysiamese_pa_t_kernel(tc, xp1, xp2, W1, b1, W2, b2, q_energy, out):
    nc = tc.nc
    with ExitStack() as ctx:
        keep = ctx.enter_context(tc.tile_pool(name="keep", bufs=1))
        work = ctx.enter_context(tc.tile_pool(name="work", bufs=2))
        ps = ctx.enter_context(tc.psum_pool(name="ps", bufs=8))
        ctx.enter_context(tc.manual_schedule())

        xv = [
            xp.rearrange("n m k -> (n m) k").rearrange("(p j) k -> p j k", j=J)
            for xp in (xp1, xp2)
        ]

        ident = keep.tile([P, P], F32, name="ident")
        make_identity(nc, ident[:])

        b1r = keep.tile([P, 4], BF16, name="b1r")
        nc.scalar.dma_start(out=b1r[:], in_=b1.rearrange("(p t) -> p t", t=4))

        ones = keep.tile([P, P], BF16, name="ones")
        nc.gpsimd.memset(ones[:], 1.0)
        b2row = keep.tile([P, Z], BF16, name="b2row")
        nc.gpsimd.memset(b2row[:], 0.0)
        w2r = keep.tile([P, 4 * Z], BF16, name="w2r")
        qr = keep.tile([P, J], BF16, name="qr")

        w1v = W1.rearrange("(c p e) f -> p c (e f)", c=4, p=P, e=2)
        w1r = keep.tile([P, 8 * F], BF16, name="w1r")
        xin = {}

        def load_x(s):
            nj, j0 = WIDTHS[s], STARTS[s]
            for a in range(2):
                xt_in = keep.tile([P, nj * E], BF16, name="x%d_%d" % (a, s))
                nc.sync.dma_start(
                    out=xt_in[:].rearrange("p (j k) -> p j k", j=nj),
                    in_=xv[a][:, j0 : j0 + nj, :],
                )
                xin[(a, s)] = xt_in

        def load_w1(g):
            nc.sync.dma_start(
                out=w1r[:, g * 2048 : (g + 1) * 2048].rearrange("p (u x) -> p u x", u=2),
                in_=w1v[:, 2 * g : 2 * g + 2, :],
            )

        load_w1(0)
        load_x(0)
        load_w1(1)
        load_x(1)
        nc.sync.dma_start(out=w2r[:], in_=W2.rearrange("(p t) z -> p (t z)", t=4))
        nc.sync.dma_start(out=b2row[0:1, :], in_=b2.rearrange("(o z) -> o z", o=1))
        for s in range(2, ROUNDS):
            load_x(s)
        nc.sync.dma_start(
            out=qr[:], in_=q_energy.rearrange("n m -> (n m)").rearrange("(p j) -> p j", j=J)
        )

        negb2 = keep.tile([P, Z], F32, name="negb2")
        w2g = keep.tile([P, 4 * Z], BF16, name="w2g", align_bytes=64)
        w2c = keep.tile([P, Z], U32, name="w2c", align_bytes=64)
        w2s = keep.tile([P, Z], U8, name="w2s", align_bytes=64)
        w1g = keep.tile([P, 8 * F], BF16, name="w1g", align_bytes=64)
        w1c = keep.tile([P, 2 * F], U32, name="w1c", align_bytes=64)
        w1s = keep.tile([P, 2 * F], U8, name="w1s", align_bytes=64)
        res = keep.tile([P, J], F32, name="res")

        def w1_regroup(eng_copy, g, t0, t1):
            dst = w1g[:, g * 2048 : (g + 1) * 2048].rearrange("p (t m j) -> p t m j", t=4, m=P, j=4)
            src = w1r[:, g * 2048 : (g + 1) * 2048].rearrange("p (j m t) -> p t m j", j=4, m=P, t=4)
            eng_copy(out=dst[:, t0:t1], in_=src[:, t0:t1])

        def w1_quant(g):
            nc.vector.quantize_mx(
                out=w1c[:, g * F : (g + 1) * F].bitcast(FP8X4),
                scales=w1s[:, g * F : (g + 1) * F],
                in_=w1g[:, g * 2048 : (g + 1) * 2048],
            )

        def layer2_constants():
            nc.vector.tensor_copy(
                out=w2g[:].rearrange("p (z t) -> p z t", t=4),
                in_=w2r[:].rearrange("p (t z) -> p z t", t=4),
            )
            b2p = ps.tile([P, 512], F32, name="bank")
            nc.tensor.matmul(b2p[:, 0:Z], lhsT=ones[:], rhs=b2row[:], start=True, stop=True)
            nc.vector.tensor_scalar(
                out=negb2[:], in0=b2p[:, 0:Z], scalar1=-1.0, scalar2=None, op0=ALU.mult
            )
            nc.vector.quantize_mx(out=w2c[:].bitcast(FP8X4), scales=w2s[:], in_=w2g[:])

        st = {}

        def banks(s):
            if WIDTHS[s] == 2:
                return [(0, 0, 0, 0), (1, 1, 0, 0), (2, 0, 1, 256), (3, 1, 1, 256)]
            return [(0, 0, None, 0), (1, 1, None, 0)]

        def transposes(s):
            for k, g, tower, _ in banks(s):
                xt = ps.tile([P, 2, 256], F32, name="bank")
                halves = [(tower, 0), (tower, 1)] if tower is not None else [(0, 0), (1, 0)]
                for h, (a, jj) in enumerate(halves):
                    xw = xin[(a, s)][:].bitcast(F32)
                    for u in range(2):
                        c0 = jj * 512 + (2 * g + u) * P
                        nc.tensor.transpose(
                            xt[:, u, h * P : (h + 1) * P], xw[:, c0 : c0 + P], ident[:]
                        )
                st[("xt", s, k)] = xt

        def x_evac(s, copies):
            cols = 256 * WIDTHS[s]
            xg = work.tile([P, 2 * 2048], BF16, name="xg", align_bytes=64)
            st[("xg", s)] = xg
            view = xg[:, 0 : 8 * cols].bitcast(F32).rearrange("p (g c u) -> p g c u", g=2, c=cols, u=2)
            for (k, g, _, c0), eng_copy in zip(banks(s), copies):
                eng_copy(
                    out=view[:, g, c0 : c0 + 256, :],
                    in_=st[("xt", s, k)][:].rearrange("p u c -> p c u"),
                )

        def x_quant(s):
            cols = 256 * WIDTHS[s]
            xc = work.tile([P, 2 * 512], U32, name="xc", align_bytes=64)
            xs = work.tile([P, 2 * 512], U8, name="xs", align_bytes=64)
            st[("xc", s)] = (xc, xs)
            nc.vector.quantize_mx(
                out=xc[:, 0 : 2 * cols].bitcast(FP8X4),
                scales=xs[:, 0 : 2 * cols],
                in_=st[("xg", s)][:, 0 : 8 * cols],
            )

        def layer1(s):
            cols = 256 * WIDTHS[s]
            xc, xs = st[("xc", s)]
            hpl = work.tile([P, 4 * 512], BF16, name="hpl")
            st[("hpl", s)] = hpl
            for t in range(4):
                hp = ps.tile([P, 512], F32, name="bank")
                for g in range(2):
                    w0 = g * F + t * P
                    nc.tensor.matmul_mx(
                        out=hp[:, 0:cols],
                        lhsT=w1c[:, w0 : w0 + P].bitcast(FP8X4),
                        lhsT_scale=w1s[:, w0 : w0 + P],
                        rhs=xc[:, g * cols : (g + 1) * cols].bitcast(FP8X4),
                        rhs_scale=xs[:, g * cols : (g + 1) * cols],
                        start=(g == 0),
                        stop=(g == 1),
                    )
                if t == 0 and WIDTHS[s] == 2:
                    nc.vector.tensor_scalar(
                        out=hpl[:, 0:cols], in0=hp[:, 0:cols],
                        scalar1=b1f[:, 0:1], scalar2=0.0, op0=ALU.add, op1=ALU.max,
                    )
                else:
                    nc.scalar.activation(
                        out=hpl[:, t * cols : (t + 1) * cols],
                        in_=hp[:, 0:cols],
                        func=ACT.Relu,
                        bias=b1r[:, t : t + 1],
                        scale=1.0,
                    )

        def h_regroup(s):
            cols = 256 * WIDTHS[s]
            hg = work.tile([P, 2048], BF16, name="hg", align_bytes=64)
            st[("hg", s)] = hg
            dst = hg[:, 0 : 4 * cols].rearrange("p (c i t) -> p c t i", i=4, t=4)
            src = st[("hpl", s)][:, 0 : 4 * cols].rearrange("p (t c i) -> p c t i", t=4, i=4)
            cut = cols // 4 if s < ROUNDS - 1 else cols // 8
            if cut < cols // 4:
                nc.scalar.copy(out=dst[:, cut:], in_=src[:, cut:])
            nc.vector.tensor_copy(out=dst[:, 0:cut], in_=src[:, 0:cut])

        def h_quant(s):
            cols = 256 * WIDTHS[s]
            hc = work.tile([P, 512], U32, name="hc", align_bytes=64)
            hs = work.tile([P, 512], U8, name="hs", align_bytes=64)
            st[("hc", s)] = (hc, hs)
            nc.vector.quantize_mx(
                out=hc[:, 0:cols].bitcast(FP8X4),
                scales=hs[:, 0:cols],
                in_=st[("hg", s)][:, 0 : 4 * cols],
            )

        def layer2(s):
            hc, hs = st[("hc", s)]
            zp = ps.tile([P, 512], F32, name="bank")
            st[("zp", s)] = zp
            for b in range(2 * WIDTHS[s]):
                nc.tensor.matmul_mx(
                    out=zp[:, b * P : (b + 1) * P],
                    lhsT=hc[:, b * P : (b + 1) * P].bitcast(FP8X4),
                    lhsT_scale=hs[:, b * P : (b + 1) * P],
                    rhs=w2c[:].bitcast(FP8X4),
                    rhs_scale=w2s[:],
                    start=True,
                    stop=True,
                )

        def z_diff(s, diff_engine):
            blocks = 2 * WIDTHS[s]
            half = WIDTHS[s] * P
            m = work.tile([P, 512], F32, name="m")
            nc.vector.tensor_tensor(
                out=m[:, 0 : 2 * half].rearrange("p (b z) -> p b z", b=blocks),
                in0=st[("zp", s)][:, 0 : 2 * half].rearrange("p (b z) -> p b z", b=blocks),
                in1=negb2[:].unsqueeze(1).to_broadcast([P, blocks, Z]),
                op=ALU.max,
            )
            d = work.tile([P, 256], F32, name="d")
            st[("d", s)] = d
            diff_engine.tensor_tensor(
                out=d[:, 0:half], in0=m[:, 0:half], in1=m[:, half : 2 * half], op=ALU.subtract
            )

        def z_square(s):
            d = st[("d", s)]
            for jj in range(WIDTHS[s]):
                junk = work.tile([P, Z], F32, name="junk")
                c = STARTS[s] + jj
                nc.scalar.activation(
                    out=junk[:],
                    in_=d[:, jj * Z : (jj + 1) * Z],
                    func=ACT.Square,
                    accum_out=res[:, c : c + 1],
                )

        def live(s):
            return 0 <= s < ROUNDS

        vcopy, scopy = nc.vector.tensor_copy, nc.scalar.copy

        def evac_engines(s):
            if s == 1:
                return [scopy, vcopy, scopy, vcopy]
            if WIDTHS[s] == 2:
                return [scopy, scopy, scopy, scopy]
            return [scopy, vcopy] if s == 0 else [scopy, scopy]

        b1f = keep.tile([P, 4], F32, name="b1f")
        nc.vector.tensor_copy(out=b1f[:], in_=b1r[:])

        w1_regroup(vcopy, 0, 0, 4)
        w1_quant(0)
        transposes(0)
        x_evac(0, evac_engines(0))
        x_quant(0)
        w1_regroup(scopy, 1, 2, 4)
        w1_regroup(vcopy, 1, 0, 2)
        w1_quant(1)

        for s in range(ROUNDS + LAG + 1):
            zs = s - LAG - 1
            if s == 1:
                layer2_constants()
            if live(zs):
                z_diff(zs, nc.gpsimd if zs < ROUNDS - 2 else nc.vector)
            if live(s - 1):
                h_regroup(s - 1)
            if live(s + 1):
                transposes(s + 1)
                x_evac(s + 1, evac_engines(s + 1))
            if live(s):
                layer1(s)
            if live(s - 1):
                h_quant(s - 1)
            if live(s + 1):
                x_quant(s + 1)
            if live(s - LAG):
                layer2(s - LAG)
            if live(zs):
                z_square(zs)

        o = keep.tile([P, J], F32, name="o")
        nc.vector.scalar_tensor_tensor(
            out=o[:], in0=res[:], scalar=1.0 / Z, in1=qr[:], op0=ALU.mult, op1=ALU.mult
        )
        nc.sync.dma_start(
            out=out.rearrange("n m -> (n m)").rearrange("(p j) -> p j", j=J), in_=o[:]
        )
